import numpy as np
import ml_dtypes


def mxq(x, axis, fmt="e4m3"):
    dtype, down = {"e4m3": (ml_dtypes.float8_e4m3fn, 7), "e5m2": (ml_dtypes.float8_e5m2, 14)}[fmt]
    v = np.moveaxis(np.asarray(x, np.float32).astype(ml_dtypes.bfloat16).astype(np.float64), axis, -1)
    blocks = v.reshape(v.shape[:-1] + (-1, 32))
    amax = np.abs(blocks).max(-1, keepdims=True)
    byte = np.maximum(np.where(amax > 0, np.frexp(amax)[1] - 1 + 127, 0) - down, 1)
    scale = np.exp2(byte - 127.0)
    codes = (blocks / scale).astype(np.float32).astype(dtype).astype(np.float64)
    return np.moveaxis((codes * scale).reshape(v.shape), -1, axis)


WIDE = False


def mx_kscale(k):
    if not WIDE:
        return np.ones(k)
    levels = np.array([10, -10, 5, -5, 0])
    a = np.random.permutation(np.resize(levels, k // 512 * 4)).reshape(k // 512, 4)
    idx = np.arange(k)
    return np.exp2(a[idx // 512, idx % 128 // 32])


BF16 = ml_dtypes.bfloat16


def bf(x):
    return np.asarray(x, np.float32).astype(BF16)


def f64(x):
    return np.asarray(x).astype(np.float64)


E2M1 = np.array([0.0, 0.5, 1.0, 1.5, 2.0, 3.0, 4.0, 6.0, -0.0, -0.5, -1.0, -1.5, -2.0, -3.0, -4.0, -6.0])


def pack_weight(w, fmt):
    k, n = w.shape
    w = f64(bf(w)).reshape(k // 32, 32, n)
    amax = np.abs(w).max(1)
    if fmt == "e4m3":
        byte = np.frexp(amax)[1] - 1 + 127 - 7
    else:
        mant, ex = np.frexp(amax / 6.0)
        byte = np.where(mant > 0.5, ex, ex - 1) + 127
    byte = np.clip(np.where(amax > 0, byte, 1), 1, 254)
    scaled = (w * np.exp2(127.0 - byte)[:, None, :]).reshape(k, n).astype(np.float32)
    by_word = np.ascontiguousarray(scaled.reshape(k // 512, 128, 4, n).transpose(0, 1, 3, 2))
    if fmt == "e4m3":
        words = by_word.astype(ml_dtypes.float8_e4m3fn).view(np.uint8)
    else:
        c = by_word.astype(ml_dtypes.float4_e2m1fn).view(np.uint8) & 0xF
        words = c[..., 0::2] | (c[..., 1::2] << 4)
    return np.ascontiguousarray(words), np.ascontiguousarray(byte.astype(np.uint8).reshape(k // 512, 16, n))


def unpack_weight(words, scales, fmt):
    g, p, n, _ = words.shape
    if fmt == "e4m3":
        vals = np.ascontiguousarray(words).view(ml_dtypes.float8_e4m3fn).astype(np.float64)
    else:
        nib = np.empty((g, p, n, 4), np.uint8)
        nib[..., 0::2] = words & 0xF
        nib[..., 1::2] = words >> 4
        vals = E2M1[nib]
    vals = vals * np.repeat(np.exp2(scales.astype(np.float64) - 127.0), 8, axis=1)[..., None]
    return vals.transpose(0, 1, 3, 2).reshape(g * 512, n)


B, I, H = 128, 2048, 1536
EPS = 1e-5
FMT = "e4m3"
assert I % 512 == 0 and H % 512 == 0


def sigmoid(v):
    return 1.0 / (1.0 + np.exp(-v))


def setup_inputs():
    s = mx_kscale(I)
    t = mx_kscale(H)
    x = bf(np.random.standard_normal((B, I)) * s)
    h = bf(np.random.standard_normal((B, H)) * t)
    c = bf(np.random.standard_normal((B, H)))
    W_ih_words, W_ih_scales = pack_weight(np.ascontiguousarray((np.random.uniform(-1.0, 1.0, (4 * H, I)) / np.sqrt(I) / s[None, :]).T), FMT)
    b_ih = bf(np.random.standard_normal(4 * H) * 0.1)
    W_hh_words, W_hh_scales = pack_weight(np.ascontiguousarray((np.random.uniform(-1.0, 1.0, (4 * H, H)) / np.sqrt(H) / t[None, :]).T), FMT)
    b_hh = bf(np.random.standard_normal(4 * H) * 0.1)
    ln_w = bf(1.0 + np.random.standard_normal(H) * 0.1)
    ln_b = bf(np.random.standard_normal(H) * 0.1)
    return {"x": x,
            "h": h,
            "c": c,
            "W_ih_words": W_ih_words,
            "W_ih_scales": W_ih_scales,
            "b_ih": b_ih,
            "W_hh_words": W_hh_words,
            "W_hh_scales": W_hh_scales,
            "b_hh": b_hh,
            "ln_w": ln_w,
            "ln_b": ln_b}


def reference(x, h, c, W_ih_words, W_ih_scales, b_ih, W_hh_words, W_hh_scales, b_hh, ln_w, ln_b):
    xw = mxq(f64(x), 1, "e4m3") @ unpack_weight(W_ih_words, W_ih_scales, FMT)
    hw = mxq(f64(h), 1, "e4m3") @ unpack_weight(W_hh_words, W_hh_scales, FMT)
    preact = xw + f64(b_ih) + hw + f64(b_hh)
    gates = sigmoid(preact[:, :3 * H])
    g_t = np.tanh(preact[:, 3 * H:])
    i_t = gates[:, :H]
    f_t = gates[:, H:2 * H]
    o_t = gates[:, 2 * H:3 * H]
    c_t = f64(c) * f_t + i_t * g_t
    mu = np.mean(c_t, axis=-1, keepdims=True)
    var = np.mean(np.square(c_t - mu), axis=-1, keepdims=True)
    c_t = (c_t - mu) / np.sqrt(var + EPS) * f64(ln_w) + f64(ln_b)
    h_t = o_t * np.tanh(c_t)
    return (h_t, c_t)

@@ -1,0 +1,263 @@
+from contextlib import ExitStack
+
+import concourse.mybir as mybir
+from concourse.masks import make_identity
+
+F32 = mybir.dt.float32
+BF16 = mybir.dt.bfloat16
+U8 = mybir.dt.uint8
+U32 = mybir.dt.uint32
+I32 = mybir.dt.int32
+FP8X4 = mybir.dt.float8_e4m3fn_x4
+ALU = mybir.AluOpType
+ACT = mybir.ActivationFunctionType
+
+P = 128
+I_DIM = 2048
+H = 1536
+EPS = 1e-5
+NT = 512
+KG_IH = 4
+KG = 7
+FLOPS = 2 * P * (I_DIM + H) * 4 * H
+
+W_BUFS = 16
+AHEAD = 14
+SCALE_QUEUE = "sync"
+
+GATE_COL = (0, H, 3 * H, 2 * H)
+
+
+def tile_lstmcelllayernorm_w_kernel(
+    tc, x, h, c, W_ih_words, W_ih_scales, b_ih, W_hh_words, W_hh_scales, b_hh, ln_w, ln_b, out_0, out_1
+):
+    nc = tc.nc
+    with ExitStack() as ctx:
+        keep = ctx.enter_context(tc.tile_pool(name="keep", bufs=1))
+        wpool = ctx.enter_context(tc.tile_pool(name="wpool", bufs=W_BUFS))
+        psum = ctx.enter_context(tc.psum_pool(name="psum", bufs=8))
+        ctx.enter_context(tc.manual_schedule())
+
+        ident = keep.tile([P, P], F32, name="ident")
+        sel = keep.tile([P, 18], BF16, name="sel")
+        vecs = keep.tile([P, NT], BF16, name="vecs")
+        nhalf = keep.tile([P, 1], F32, name="nhalf")
+        xh = keep.tile([P, I_DIM + H], BF16, name="xh")
+        grouped = keep.tile([P, I_DIM + H], BF16, name="grouped", align_bytes=64)
+        codes = keep.tile([P, KG * P], U32, name="codes", align_bytes=64)
+        xs = keep.tile([P, KG * P], U8, name="xs", align_bytes=64)
+        planes_ih = keep.tile([P, 4 * H], U8, name="planes_ih", align_bytes=64)
+        planes_hh = keep.tile([P, 4 * H], U8, name="planes_hh", align_bytes=64)
+        bcast = keep.tile([P, 18 * NT], F32, name="bcast")
+        c_sb = keep.tile([P, H], BF16, name="c_sb")
+        gi = keep.tile([P, H], F32, name="gi")
+        gf = keep.tile([P, H], F32, name="gf")
+        gg = keep.tile([P, H], F32, name="gg")
+        go = keep.tile([P, H], F32, name="go")
+        tn = keep.tile([P, H], F32, name="tn")
+        ct = keep.tile([P, H], F32, name="ct")
+        th = keep.tile([P, H], F32, name="th")
+        stats = keep.tile([P, 3, 6], F32, name="stats")
+        mv = keep.tile([P, 2], F32, name="mv")
+        ve = keep.tile([P, 1], F32, name="ve")
+        rstd = keep.tile([P, 1], F32, name="rstd")
+
+        nc.sync.dma_start(out=xh[:, 0:I_DIM], in_=x)
+        nc.sync.dma_start(out=xh[:, I_DIM : I_DIM + H], in_=h)
+
+        nc.vector.memset(vecs[:], 0.0)
+        nc.vector.memset(planes_ih[:].bitcast(I32), 0)
+        nc.vector.memset(planes_hh[:].bitcast(I32), 0)
+        make_identity(nc, ident[:])
+        nc.gpsimd.memset(nhalf[:], -0.5)
+
+        nc.scalar.dma_start(out=vecs[0:12, :], in_=b_ih.rearrange("(r n) -> r n", r=12))
+        nc.scalar.dma_start(out=vecs[12:24, :], in_=b_hh.rearrange("(r n) -> r n", r=12))
+        nc.scalar.dma_start(out=vecs[24:27, :], in_=ln_w.rearrange("(r n) -> r n", r=3))
+        nc.scalar.dma_start(out=vecs[27:30, :], in_=ln_b.rearrange("(r n) -> r n", r=3))
+
+        for q in range(4):
+            if SCALE_QUEUE == "sync":
+                nc.sync.dma_start(
+                    out=planes_ih[32 * q : 32 * q + 16, :].bitcast(I32),
+                    in_=W_ih_scales[:, 4 * q : 4 * q + 4, :].bitcast(I32),
+                )
+                nc.sync.dma_start(
+                    out=planes_hh[32 * q : 32 * q + 12, :].bitcast(I32),
+                    in_=W_hh_scales[:, 4 * q : 4 * q + 4, :].bitcast(I32),
+                )
+            else:
+                nc.gpsimd.dma_start(
+                    out=planes_ih[32 * q : 32 * q + 16, :].bitcast(F32),
+                    in_=W_ih_scales[:, 4 * q : 4 * q + 4, :].bitcast(F32),
+                )
+                nc.gpsimd.dma_start(
+                    out=planes_hh[32 * q : 32 * q + 12, :].bitcast(F32),
+                    in_=W_hh_scales[:, 4 * q : 4 * q + 4, :].bitcast(F32),
+                )
+        nc.sync.dma_start(out=c_sb[:], in_=c)
+
+        loads = []
+        for ph in range(4):
+            for kg in range(KG):
+                if ph == 3 and kg == KG - 1:
+                    for j in range(3):
+                        loads.append((ph, kg, NT * j, NT))
+                else:
+                    loads.append((ph, kg, 0, H))
+        w_tiles = {}
+
+        def issue(n):
+            ph, kg, c0, width = loads[n]
+            words = W_ih_words[kg] if kg < KG_IH else W_hh_words[kg - KG_IH]
+            flat = words.rearrange("p n t -> p (n t)")
+            n0 = GATE_COL[ph] + c0
+            w = wpool.tile([P, H], U32, name="w", tag="w", align_bytes=64)
+            nc.sync.dma_start(
+                out=w[:, 0:width].bitcast(I32),
+                in_=flat[:, 4 * n0 : 4 * (n0 + width)].bitcast(I32),
+            )
+            w_tiles[n] = w
+
+        for n in range(AHEAD):
+            issue(n)
+
+        nc.vector.tensor_tensor(out=sel[:, 0:12], in0=ident[:, 0:12], in1=ident[:, 12:24], op=ALU.add)
+        nc.vector.tensor_copy(out=sel[:, 12:18], in_=ident[:, 24:30])
+
+        xw = xh[:].bitcast(F32)
+        gw = grouped[:].bitcast(F32)
+        tps = []
+        for pr in range(4):
+            tp = psum.tile([P, NT], F32, name="tp", tag="ps")
+            tps.append(tp)
+            for gl in range(2):
+                g = 2 * pr + gl
+                if g < KG:
+                    for u in range(2):
+                        nc.tensor.transpose(
+                            out=tp[:, 256 * gl + 128 * u : 256 * gl + 128 * u + 128],
+                            in_=xw[:, 256 * g + u : 256 * (g + 1) : 2],
+                            identity=ident[:],
+                        )
+
+        def regroup(pr):
+            ng = 2 if pr < 3 else 1
+            nc.vector.tensor_copy(
+                out=gw[:, 512 * pr : 512 * pr + 256 * ng].rearrange("p (g m u) -> p g m u", g=ng, u=2),
+                in_=tps[pr][:, 0 : 256 * ng].rearrange("p (g u m) -> p g m u", g=ng, u=2),
+            )
+
+        def quantise(g0, ng):
+            nc.vector.quantize_mx(
+                out=codes[:, P * g0 : P * (g0 + ng)].bitcast(FP8X4),
+                scales=xs[:, P * g0 : P * (g0 + ng)],
+                in_=grouped[:, NT * g0 : NT * (g0 + ng)],
+            )
+
+        regroup(0)
+        regroup(1)
+        regroup(2)
+        quantise(0, 4)
+        regroup(3)
+        quantise(4, 2)
+        quantise(6, 1)
+
+        def spread(js):
+            for j in js:
+                ps = psum.tile([P, NT], F32, name="ps", tag="ps")
+                nc.tensor.matmul(
+                    out=ps[:],
+                    lhsT=sel[:, j : j + 1].to_broadcast([P, P]),
+                    rhs=vecs[:],
+                    start=True,
+                    stop=True,
+                )
+                nc.scalar.copy(out=bcast[:, NT * j : NT * (j + 1)], in_=ps[:])
+
+        spread([0, 1, 2])
+        extras = {
+            (0, 2): [3, 4, 5],
+            (1, 2): [9, 10, 11],
+            (1, 4): [12, 13, 14],
+            (2, 1): [15, 16, 17],
+            (2, 3): [6, 7, 8],
+        }
+        lnw = bcast[:, 12 * NT : 15 * NT]
+        lnb = bcast[:, 15 * NT : 18 * NT]
+
+        def cols(j):
+            return slice(NT * j, NT * (j + 1))
+
+        def preact(ph, j, acc, dst, func):
+            n0 = GATE_COL[ph] + NT * j
+            nc.vector.tensor_tensor(out=dst[:, cols(j)], in0=acc[:], in1=bcast[:, n0 : n0 + NT], op=ALU.add)
+            nc.scalar.activation(out=dst[:, cols(j)], in_=dst[:, cols(j)], func=func)
+
+        issued = AHEAD
+        accs = []
+        for n in range(len(loads)):
+            ph, kg, c0, width = loads[n]
+            if issued < len(loads):
+                issue(issued)
+                issued += 1
+            if kg == 0:
+                accs = []
+                for j in range(3):
+                    acc = psum.tile([P, NT], F32, name="acc", tag="ps")
+                    accs.append(acc)
+            w = w_tiles[n]
+            planes = planes_ih if kg < KG_IH else planes_hh
+            k_off = 4 * (kg % KG_IH)
+            for j in range(c0 // NT, (c0 + width) // NT):
+                n0 = GATE_COL[ph] + NT * j
+                nc.tensor.matmul_mx(
+                    out=accs[j][:],
+                    lhsT=codes[:, P * kg : P * (kg + 1)].bitcast(FP8X4),
+                    lhsT_scale=xs[:, P * kg : P * (kg + 1)],
+                    rhs=w[:, NT * j - c0 : NT * (j + 1) - c0].bitcast(FP8X4),
+                    rhs_scale=planes[k_off:P, n0 : n0 + NT],
+                    start=(kg == 0),
+                    stop=(kg == KG - 1),
+                )
+                if ph == 3 and kg == KG - 1:
+                    preact(3, j, accs[j], go, ACT.Sigmoid)
+            if (ph, kg) in extras:
+                spread(extras[(ph, kg)])
+            if kg < KG - 1:
+                continue
+            if ph == 0:
+                for j in range(3):
+                    preact(0, j, accs[j], gi, ACT.Sigmoid)
+            elif ph == 1:
+                for j in range(3):
+                    preact(1, j, accs[j], gf, ACT.Sigmoid)
+                for j in range(3):
+                    nc.vector.tensor_tensor(out=gf[:, cols(j)], in0=gf[:, cols(j)], in1=c_sb[:, cols(j)], op=ALU.mult)
+            elif ph == 2:
+                for j in range(3):
+                    preact(2, j, accs[j], gg, ACT.Tanh)
+                for j in range(3):
+                    nc.vector.tensor_tensor(out=gg[:, cols(j)], in0=gg[:, cols(j)], in1=gi[:, cols(j)], op=ALU.mult)
+                    nc.vector.tensor_tensor(out=gg[:, cols(j)], in0=gg[:, cols(j)], in1=gf[:, cols(j)], op=ALU.add)
+                    nc.vector.bn_stats(out=stats[:, j, :], in_=gg[:, cols(j)])
+                nc.vector.bn_aggr(out=mv[:], in_=stats[:].rearrange("p a b -> p (a b)"))
+                nc.vector.tensor_scalar(out=ve[:], in0=mv[:, 1:2], scalar1=EPS, scalar2=None, op0=ALU.add)
+                nc.gpsimd.tensor_tensor(out=rstd[:], in0=ve[:], in1=nhalf[:], op=ALU.pow)
+                nc.vector.scalar_tensor_tensor(
+                    out=tn[:], in0=gg[:], scalar=mv[:, 0:1], in1=lnw, op0=ALU.subtract, op1=ALU.mult
+                )
+                for j in range(3):
+                    nc.vector.scalar_tensor_tensor(
+                        out=ct[:, cols(j)],
+                        in0=tn[:, cols(j)],
+                        scalar=rstd[:, 0:1],
+                        in1=lnb[:, cols(j)],
+                        op0=ALU.mult,
+                        op1=ALU.add,
+                    )
+                    nc.scalar.activation(out=th[:, cols(j)], in_=ct[:, cols(j)], func=ACT.Tanh)
+                nc.sync.dma_start(out=out_1, in_=ct[:])
+        for j in range(3):
+            nc.vector.tensor_tensor(out=go[:, cols(j)], in0=go[:, cols(j)], in1=th[:, cols(j)], op=ALU.mult)
+            nc.sync.dma_start(out=out_0[:, cols(j)], in_=go[:, cols(j)])

@@ -23,7 +23,6 @@ FLOPS = 2 * P * (I_DIM + H) * 4 * H
 
 W_BUFS = 16
 AHEAD = 14
-SCALE_QUEUE = "sync"
 
 GATE_COL = (0, H, 3 * H, 2 * H)
 
@@ -77,24 +76,15 @@ def tile_lstmcelllayernorm_w_kernel(
         nc.scalar.dma_start(out=vecs[27:30, :], in_=ln_b.rearrange("(r n) -> r n", r=3))
 
         for q in range(4):
-            if SCALE_QUEUE == "sync":
-                nc.sync.dma_start(
-                    out=planes_ih[32 * q : 32 * q + 16, :].bitcast(I32),
-                    in_=W_ih_scales[:, 4 * q : 4 * q + 4, :].bitcast(I32),
-                )
-                nc.sync.dma_start(
-                    out=planes_hh[32 * q : 32 * q + 12, :].bitcast(I32),
-                    in_=W_hh_scales[:, 4 * q : 4 * q + 4, :].bitcast(I32),
-                )
-            else:
-                nc.gpsimd.dma_start(
-                    out=planes_ih[32 * q : 32 * q + 16, :].bitcast(F32),
-                    in_=W_ih_scales[:, 4 * q : 4 * q + 4, :].bitcast(F32),
-                )
-                nc.gpsimd.dma_start(
-                    out=planes_hh[32 * q : 32 * q + 12, :].bitcast(F32),
-                    in_=W_hh_scales[:, 4 * q : 4 * q + 4, :].bitcast(F32),
-                )
+            nc.gpsimd.dma_start(
+                out=planes_ih[32 * q : 32 * q + 16, :].bitcast(F32),
+                in_=W_ih_scales[:, 4 * q : 4 * q + 4, :].bitcast(F32),
+            )
+        for q in range(4):
+            nc.gpsimd.dma_start(
+                out=planes_hh[32 * q : 32 * q + 12, :].bitcast(F32),
+                in_=W_hh_scales[:, 4 * q : 4 * q + 4, :].bitcast(F32),
+            )
         nc.sync.dma_start(out=c_sb[:], in_=c)
 
         loads = []

@@ -23,6 +23,7 @@ FLOPS = 2 * P * (I_DIM + H) * 4 * H
 
 W_BUFS = 16
 AHEAD = 14
+CHUNKED = (0, 0, 2, 1)
 
 GATE_COL = (0, H, 3 * H, 2 * H)
 
@@ -75,26 +76,32 @@ def tile_lstmcelllayernorm_w_kernel(
         nc.scalar.dma_start(out=vecs[24:27, :], in_=ln_w.rearrange("(r n) -> r n", r=3))
         nc.scalar.dma_start(out=vecs[27:30, :], in_=ln_b.rearrange("(r n) -> r n", r=3))
 
+        def load_scales(q, planes, scales, rows):
+            if q < 2:
+                nc.sync.dma_start(
+                    out=planes[32 * q : 32 * q + rows, :].bitcast(I32),
+                    in_=scales[:, 4 * q : 4 * q + 4, :].bitcast(I32),
+                )
+            else:
+                nc.gpsimd.dma_start(
+                    out=planes[32 * q : 32 * q + rows, :].bitcast(F32),
+                    in_=scales[:, 4 * q : 4 * q + 4, :].bitcast(F32),
+                )
+
         for q in range(4):
-            nc.gpsimd.dma_start(
-                out=planes_ih[32 * q : 32 * q + 16, :].bitcast(F32),
-                in_=W_ih_scales[:, 4 * q : 4 * q + 4, :].bitcast(F32),
-            )
+            load_scales(q, planes_ih, W_ih_scales, 16)
         for q in range(4):
-            nc.gpsimd.dma_start(
-                out=planes_hh[32 * q : 32 * q + 12, :].bitcast(F32),
-                in_=W_hh_scales[:, 4 * q : 4 * q + 4, :].bitcast(F32),
-            )
+            load_scales(q, planes_hh, W_hh_scales, 12)
         nc.sync.dma_start(out=c_sb[:], in_=c)
 
         loads = []
         for ph in range(4):
-            for kg in range(KG):
-                if ph == 3 and kg == KG - 1:
-                    for j in range(3):
-                        loads.append((ph, kg, NT * j, NT))
-                else:
-                    loads.append((ph, kg, 0, H))
+            whole = KG - CHUNKED[ph]
+            for kg in range(whole):
+                loads.append((ph, kg, 0, H))
+            for j in range(3):
+                for kg in range(whole, KG):
+                    loads.append((ph, kg, NT * j, NT))
         w_tiles = {}
 
         def issue(n):
@@ -184,6 +191,11 @@ def tile_lstmcelllayernorm_w_kernel(
             nc.vector.tensor_tensor(out=dst[:, cols(j)], in0=acc[:], in1=bcast[:, n0 : n0 + NT], op=ALU.add)
             nc.scalar.activation(out=dst[:, cols(j)], in_=dst[:, cols(j)], func=func)
 
+        def cell(j):
+            nc.vector.tensor_tensor(out=gg[:, cols(j)], in0=gg[:, cols(j)], in1=gi[:, cols(j)], op=ALU.mult)
+            nc.vector.tensor_tensor(out=gg[:, cols(j)], in0=gg[:, cols(j)], in1=gf[:, cols(j)], op=ALU.add)
+            nc.vector.bn_stats(out=stats[:, j, :], in_=gg[:, cols(j)])
+
         issued = AHEAD
         accs = []
         for n in range(len(loads)):
@@ -212,9 +224,15 @@ def tile_lstmcelllayernorm_w_kernel(
                 )
                 if ph == 3 and kg == KG - 1:
                     preact(3, j, accs[j], go, ACT.Sigmoid)
+                if ph == 2 and kg == KG - 1:
+                    preact(2, j, accs[j], gg, ACT.Tanh)
+                    if j > 0:
+                        cell(j - 1)
+                    if j == 2:
+                        cell(2)
             if (ph, kg) in extras:
                 spread(extras[(ph, kg)])
-            if kg < KG - 1:
+            if n + 1 < len(loads) and loads[n + 1][0] == ph:
                 continue
             if ph == 0:
                 for j in range(3):
@@ -225,12 +243,6 @@ def tile_lstmcelllayernorm_w_kernel(
                 for j in range(3):
                     nc.vector.tensor_tensor(out=gf[:, cols(j)], in0=gf[:, cols(j)], in1=c_sb[:, cols(j)], op=ALU.mult)
             elif ph == 2:
-                for j in range(3):
-                    preact(2, j, accs[j], gg, ACT.Tanh)
-                for j in range(3):
-                    nc.vector.tensor_tensor(out=gg[:, cols(j)], in0=gg[:, cols(j)], in1=gi[:, cols(j)], op=ALU.mult)
-                    nc.vector.tensor_tensor(out=gg[:, cols(j)], in0=gg[:, cols(j)], in1=gf[:, cols(j)], op=ALU.add)
-                    nc.vector.bn_stats(out=stats[:, j, :], in_=gg[:, cols(j)])
                 nc.vector.bn_aggr(out=mv[:], in_=stats[:].rearrange("p a b -> p (a b)"))
                 nc.vector.tensor_scalar(out=ve[:], in0=mv[:, 1:2], scalar1=EPS, scalar2=None, op0=ALU.add)
                 nc.gpsimd.tensor_tensor(out=rstd[:], in0=ve[:], in1=nhalf[:], op=ALU.pow)

@@ -23,7 +23,7 @@ FLOPS = 2 * P * (I_DIM + H) * 4 * H
 
 W_BUFS = 16
 AHEAD = 14
-CHUNKED = (0, 0, 2, 1)
+CHUNKED = (0, 0, 4, 1)
 
 GATE_COL = (0, H, 3 * H, 2 * H)
 
@@ -175,10 +175,10 @@ def tile_lstmcelllayernorm_w_kernel(
         spread([0, 1, 2])
         extras = {
             (0, 2): [3, 4, 5],
-            (1, 2): [9, 10, 11],
-            (1, 4): [12, 13, 14],
-            (2, 1): [15, 16, 17],
-            (2, 3): [6, 7, 8],
+            (0, 4): [9, 10, 11],
+            (1, 1): [12, 13, 14],
+            (1, 3): [15, 16, 17],
+            (1, 5): [6, 7, 8],
         }
         lnw = bcast[:, 12 * NT : 15 * NT]
         lnb = bcast[:, 15 * NT : 18 * NT]

@@ -21,11 +21,13 @@ KG_IH = 4
 KG = 7
 FLOPS = 2 * P * (I_DIM + H) * 4 * H
 
-W_BUFS = 16
-AHEAD = 14
-CHUNKED = (0, 0, 4, 1)
+COL_I = 0
+COL_F = H
+COL_O = 2 * H
+COL_G = 3 * H
 
-GATE_COL = (0, H, 3 * H, 2 * H)
+G_CHUNKED = 4
+W_BUFS = {2 * H: 4, H: 3, 2 * NT: 5, NT: 10, NT // 2: 2}
 
 
 def tile_lstmcelllayernorm_w_kernel(
@@ -34,7 +36,8 @@ def tile_lstmcelllayernorm_w_kernel(
     nc = tc.nc
     with ExitStack() as ctx:
         keep = ctx.enter_context(tc.tile_pool(name="keep", bufs=1))
-        wpool = ctx.enter_context(tc.tile_pool(name="wpool", bufs=W_BUFS))
+        work = ctx.enter_context(tc.tile_pool(name="work", bufs=5))
+        wpool = ctx.enter_context(tc.tile_pool(name="wpool", bufs=1))
         psum = ctx.enter_context(tc.psum_pool(name="psum", bufs=8))
         ctx.enter_context(tc.manual_schedule())
 
@@ -50,13 +53,6 @@ def tile_lstmcelllayernorm_w_kernel(
         planes_hh = keep.tile([P, 4 * H], U8, name="planes_hh", align_bytes=64)
         bcast = keep.tile([P, 18 * NT], F32, name="bcast")
         c_sb = keep.tile([P, H], BF16, name="c_sb")
-        gi = keep.tile([P, H], F32, name="gi")
-        gf = keep.tile([P, H], F32, name="gf")
-        gg = keep.tile([P, H], F32, name="gg")
-        go = keep.tile([P, H], F32, name="go")
-        tn = keep.tile([P, H], F32, name="tn")
-        ct = keep.tile([P, H], F32, name="ct")
-        th = keep.tile([P, H], F32, name="th")
         stats = keep.tile([P, 3, 6], F32, name="stats")
         mv = keep.tile([P, 2], F32, name="mv")
         ve = keep.tile([P, 1], F32, name="ve")
@@ -94,30 +90,42 @@ def tile_lstmcelllayernorm_w_kernel(
             load_scales(q, planes_hh, W_hh_scales, 12)
         nc.sync.dma_start(out=c_sb[:], in_=c)
 
-        loads = []
-        for ph in range(4):
-            whole = KG - CHUNKED[ph]
-            for kg in range(whole):
-                loads.append((ph, kg, 0, H))
-            for j in range(3):
-                for kg in range(whole, KG):
-                    loads.append((ph, kg, NT * j, NT))
+        steps = []
+        for kg in range(KG):
+            steps.append((kg, COL_I, 2 * H))
+        for kg in range(KG - G_CHUNKED):
+            steps.append((kg, COL_G, H))
+        for j in range(3):
+            for kg in range(KG - G_CHUNKED, KG):
+                steps.append((kg, COL_G + NT * j, NT))
+        for kg in range(KG):
+            steps.append((kg, COL_O, 2 * NT))
+        for kg in range(KG - 1):
+            steps.append((kg, COL_O + 2 * NT, NT))
+        for half in range(2):
+            steps.append((KG - 1, COL_O + 2 * NT + (NT // 2) * half, NT // 2))
+
         w_tiles = {}
+        taken = {}
+        for width in W_BUFS:
+            taken[width] = []
+        issued = [0]
 
-        def issue(n):
-            ph, kg, c0, width = loads[n]
-            words = W_ih_words[kg] if kg < KG_IH else W_hh_words[kg - KG_IH]
-            flat = words.rearrange("p n t -> p (n t)")
-            n0 = GATE_COL[ph] + c0
-            w = wpool.tile([P, H], U32, name="w", tag="w", align_bytes=64)
-            nc.sync.dma_start(
-                out=w[:, 0:width].bitcast(I32),
-                in_=flat[:, 4 * n0 : 4 * (n0 + width)].bitcast(I32),
-            )
-            w_tiles[n] = w
+        def prefetch(n):
+            for m in range(issued[0], len(steps)):
+                kg, n0, width = steps[m]
+                before = taken[width]
+                if len(before) >= W_BUFS[width] and before[len(before) - W_BUFS[width]] >= n:
+                    break
+                words = W_ih_words[kg] if kg < KG_IH else W_hh_words[kg - KG_IH]
+                flat = words.rearrange("p n t -> p (n t)")
+                w = wpool.tile([P, width], U32, name="w%d" % width, tag="w%d" % width, bufs=W_BUFS[width], align_bytes=64)
+                nc.sync.dma_start(out=w[:].bitcast(I32), in_=flat[:, 4 * n0 : 4 * (n0 + width)].bitcast(I32))
+                w_tiles[m] = w
+                before.append(m)
+                issued[0] = m + 1
 
-        for n in range(AHEAD):
-            issue(n)
+        prefetch(0)
 
         nc.vector.tensor_tensor(out=sel[:, 0:12], in0=ident[:, 0:12], in1=ident[:, 12:24], op=ALU.add)
         nc.vector.tensor_copy(out=sel[:, 12:18], in_=ident[:, 24:30])
@@ -172,94 +180,114 @@ def tile_lstmcelllayernorm_w_kernel(
                 )
                 nc.scalar.copy(out=bcast[:, NT * j : NT * (j + 1)], in_=ps[:])
 
-        spread([0, 1, 2])
-        extras = {
-            (0, 2): [3, 4, 5],
-            (0, 4): [9, 10, 11],
-            (1, 1): [12, 13, 14],
-            (1, 3): [15, 16, 17],
-            (1, 5): [6, 7, 8],
-        }
+        spread([0, 1, 2, 3, 4, 5])
+        extras = {1: [9, 10, 11], 2: [12, 13, 14], 3: [15, 16, 17], 4: [6, 7, 8]}
         lnw = bcast[:, 12 * NT : 15 * NT]
         lnb = bcast[:, 15 * NT : 18 * NT]
 
+        def widths_of(n0):
+            return NT // 2 if n0 >= COL_O + 2 * NT and n0 < COL_G else NT
+
+        def preact(n0, dst, first, func):
+            wd = widths_of(n0)
+            d = dst[:, n0 - first : n0 - first + wd]
+            nc.vector.tensor_tensor(out=d, in0=accs[n0][:, 0:wd], in1=bcast[:, n0 : n0 + wd], op=ALU.add)
+            nc.scalar.activation(out=d, in_=d, func=func)
+
         def cols(j):
             return slice(NT * j, NT * (j + 1))
-
-        def preact(ph, j, acc, dst, func):
-            n0 = GATE_COL[ph] + NT * j
-            nc.vector.tensor_tensor(out=dst[:, cols(j)], in0=acc[:], in1=bcast[:, n0 : n0 + NT], op=ALU.add)
-            nc.scalar.activation(out=dst[:, cols(j)], in_=dst[:, cols(j)], func=func)
 
         def cell(j):
             nc.vector.tensor_tensor(out=gg[:, cols(j)], in0=gg[:, cols(j)], in1=gi[:, cols(j)], op=ALU.mult)
             nc.vector.tensor_tensor(out=gg[:, cols(j)], in0=gg[:, cols(j)], in1=gf[:, cols(j)], op=ALU.add)
             nc.vector.bn_stats(out=stats[:, j, :], in_=gg[:, cols(j)])
 
-        issued = AHEAD
-        accs = []
-        for n in range(len(loads)):
-            ph, kg, c0, width = loads[n]
-            if issued < len(loads):
-                issue(issued)
-                issued += 1
-            if kg == 0:
-                accs = []
-                for j in range(3):
-                    acc = psum.tile([P, NT], F32, name="acc", tag="ps")
-                    accs.append(acc)
+        def hidden(c0, wd):
+            nc.vector.tensor_tensor(out=go[:, c0 : c0 + wd], in0=go[:, c0 : c0 + wd], in1=th[:, c0 : c0 + wd], op=ALU.mult)
+            nc.sync.dma_start(out=out_0[:, c0 : c0 + wd], in_=go[:, c0 : c0 + wd])
+
+        gi = work.tile([P, H], F32, name="gi", tag="work")
+        gf = work.tile([P, H], F32, name="gf", tag="work")
+        gg = work.tile([P, H], F32, name="gg", tag="work")
+        tn = work.tile([P, H], F32, name="tn", tag="work")
+        ct = work.tile([P, H], F32, name="ct", tag="work")
+        th = None
+        go = None
+
+        accs = {}
+        ct_stored = False
+        for n in range(len(steps)):
+            kg, first, width = steps[n]
+            prefetch(n)
+            if issued[0] == len(steps) and th is not None and not ct_stored:
+                nc.sync.dma_start(out=out_1, in_=ct[:])
+                ct_stored = True
             w = w_tiles[n]
             planes = planes_ih if kg < KG_IH else planes_hh
             k_off = 4 * (kg % KG_IH)
-            for j in range(c0 // NT, (c0 + width) // NT):
-                n0 = GATE_COL[ph] + NT * j
+            n0 = first
+            done = []
+            for rep in range(12):
+                if n0 >= first + width:
+                    break
+                wd = widths_of(n0)
+                if kg == 0:
+                    acc = psum.tile([P, NT], F32, name="acc", tag="ps")
+                    accs[n0] = acc
                 nc.tensor.matmul_mx(
-                    out=accs[j][:],
+                    out=accs[n0][:, 0:wd],
                     lhsT=codes[:, P * kg : P * (kg + 1)].bitcast(FP8X4),
                     lhsT_scale=xs[:, P * kg : P * (kg + 1)],
-                    rhs=w[:, NT * j - c0 : NT * (j + 1) - c0].bitcast(FP8X4),
-                    rhs_scale=planes[k_off:P, n0 : n0 + NT],
+                    rhs=w[:, n0 - first : n0 - first + wd].bitcast(FP8X4),
+                    rhs_scale=planes[k_off:P, n0 : n0 + wd],
                     start=(kg == 0),
                     stop=(kg == KG - 1),
                 )
-                if ph == 3 and kg == KG - 1:
-                    preact(3, j, accs[j], go, ACT.Sigmoid)
-                if ph == 2 and kg == KG - 1:
-                    preact(2, j, accs[j], gg, ACT.Tanh)
-                    if j > 0:
-                        cell(j - 1)
-                    if j == 2:
-                        cell(2)
-            if (ph, kg) in extras:
-                spread(extras[(ph, kg)])
-            if n + 1 < len(loads) and loads[n + 1][0] == ph:
+                if kg == KG - 1:
+                    done.append(n0)
+                n0 += wd
+            if first == COL_I and kg in extras:
+                spread(extras[kg])
+            if len(done) == 0:
                 continue
-            if ph == 0:
-                for j in range(3):
-                    preact(0, j, accs[j], gi, ACT.Sigmoid)
-            elif ph == 1:
-                for j in range(3):
-                    preact(1, j, accs[j], gf, ACT.Sigmoid)
+            if first == COL_I:
+                for m0 in done:
+                    if m0 < COL_F:
+                        preact(m0, gi, COL_I, ACT.Sigmoid)
+                    else:
+                        preact(m0, gf, COL_F, ACT.Sigmoid)
                 for j in range(3):
                     nc.vector.tensor_tensor(out=gf[:, cols(j)], in0=gf[:, cols(j)], in1=c_sb[:, cols(j)], op=ALU.mult)
-            elif ph == 2:
-                nc.vector.bn_aggr(out=mv[:], in_=stats[:].rearrange("p a b -> p (a b)"))
-                nc.vector.tensor_scalar(out=ve[:], in0=mv[:, 1:2], scalar1=EPS, scalar2=None, op0=ALU.add)
-                nc.gpsimd.tensor_tensor(out=rstd[:], in0=ve[:], in1=nhalf[:], op=ALU.pow)
-                nc.vector.scalar_tensor_tensor(
-                    out=tn[:], in0=gg[:], scalar=mv[:, 0:1], in1=lnw, op0=ALU.subtract, op1=ALU.mult
-                )
-                for j in range(3):
+            elif first >= COL_G:
+                j = (first - COL_G) // NT
+                preact(first, gg, COL_G, ACT.Tanh)
+                if j > 0:
+                    cell(j - 1)
+                if j == 2:
+                    cell(2)
+                    nc.vector.bn_aggr(out=mv[:], in_=stats[:].rearrange("p a b -> p (a b)"))
+                    nc.vector.tensor_scalar(out=ve[:], in0=mv[:, 1:2], scalar1=EPS, scalar2=None, op0=ALU.add)
+                    nc.gpsimd.tensor_tensor(out=rstd[:], in0=ve[:], in1=nhalf[:], op=ALU.pow)
                     nc.vector.scalar_tensor_tensor(
-                        out=ct[:, cols(j)],
-                        in0=tn[:, cols(j)],
-                        scalar=rstd[:, 0:1],
-                        in1=lnb[:, cols(j)],
-                        op0=ALU.mult,
-                        op1=ALU.add,
+                        out=tn[:], in0=gg[:], scalar=mv[:, 0:1], in1=lnw, op0=ALU.subtract, op1=ALU.mult
                     )
-                    nc.scalar.activation(out=th[:, cols(j)], in_=ct[:, cols(j)], func=ACT.Tanh)
-                nc.sync.dma_start(out=out_1, in_=ct[:])
-        for j in range(3):
-            nc.vector.tensor_tensor(out=go[:, cols(j)], in0=go[:, cols(j)], in1=th[:, cols(j)], op=ALU.mult)
-            nc.sync.dma_start(out=out_0[:, cols(j)], in_=go[:, cols(j)])
+                    th = work.tile([P, H], F32, name="th", tag="work")
+                    go = work.tile([P, H], F32, name="go", tag="work")
+                    for jj in range(3):
+                        nc.vector.scalar_tensor_tensor(
+                            out=ct[:, cols(jj)],
+                            in0=tn[:, cols(jj)],
+                            scalar=rstd[:, 0:1],
+                            in1=lnb[:, cols(jj)],
+                            op0=ALU.mult,
+                            op1=ALU.add,
+                        )
+                        nc.scalar.activation(out=th[:, cols(jj)], in_=ct[:, cols(jj)], func=ACT.Tanh)
+            else:
+                for m0 in done:
+                    preact(m0, go, COL_O, ACT.Sigmoid)
+                if first == COL_O:
+                    hidden(0, NT)
+                    hidden(NT, NT)
+        hidden(2 * NT, NT // 2)
+        hidden(2 * NT + NT // 2, NT // 2)

@@ -39,7 +39,6 @@ def tile_lstmcelllayernorm_w_kernel(
         work = ctx.enter_context(tc.tile_pool(name="work", bufs=5))
         wpool = ctx.enter_context(tc.tile_pool(name="wpool", bufs=1))
         psum = ctx.enter_context(tc.psum_pool(name="psum", bufs=8))
-        ctx.enter_context(tc.manual_schedule())
 
         ident = keep.tile([P, P], F32, name="ident")
         sel = keep.tile([P, 18], BF16, name="sel")

@@ -26,8 +26,8 @@ COL_F = H
 COL_O = 2 * H
 COL_G = 3 * H
 
-G_CHUNKED = 4
-W_BUFS = {2 * H: 4, H: 3, 2 * NT: 5, NT: 10, NT // 2: 2}
+IF_JOINT = 5
+W_BUFS = {2 * H: 4, H: 4, 2 * NT: 5, NT: 10, NT // 2: 2}
 
 
 def tile_lstmcelllayernorm_w_kernel(
@@ -90,12 +90,14 @@ def tile_lstmcelllayernorm_w_kernel(
         nc.sync.dma_start(out=c_sb[:], in_=c)
 
         steps = []
-        for kg in range(KG):
+        for kg in range(IF_JOINT):
             steps.append((kg, COL_I, 2 * H))
-        for kg in range(KG - G_CHUNKED):
-            steps.append((kg, COL_G, H))
+        for kg in range(IF_JOINT, KG):
+            steps.append((kg, COL_I, H))
+        for kg in range(IF_JOINT, KG):
+            steps.append((kg, COL_F, H))
         for j in range(3):
-            for kg in range(KG - G_CHUNKED, KG):
+            for kg in range(KG):
                 steps.append((kg, COL_G + NT * j, NT))
         for kg in range(KG):
             steps.append((kg, COL_O, 2 * NT))
@@ -251,19 +253,17 @@ def tile_lstmcelllayernorm_w_kernel(
                 continue
             if first == COL_I:
                 for m0 in done:
-                    if m0 < COL_F:
-                        preact(m0, gi, COL_I, ACT.Sigmoid)
-                    else:
-                        preact(m0, gf, COL_F, ACT.Sigmoid)
+                    preact(m0, gi, COL_I, ACT.Sigmoid)
+            elif first == COL_F:
+                for m0 in done:
+                    preact(m0, gf, COL_F, ACT.Sigmoid)
                 for j in range(3):
                     nc.vector.tensor_tensor(out=gf[:, cols(j)], in0=gf[:, cols(j)], in1=c_sb[:, cols(j)], op=ALU.mult)
             elif first >= COL_G:
                 j = (first - COL_G) // NT
                 preact(first, gg, COL_G, ACT.Tanh)
-                if j > 0:
-                    cell(j - 1)
+                cell(j)
                 if j == 2:
-                    cell(2)
                     nc.vector.bn_aggr(out=mv[:], in_=stats[:].rearrange("p a b -> p (a b)"))
                     nc.vector.tensor_scalar(out=ve[:], in0=mv[:, 1:2], scalar1=EPS, scalar2=None, op0=ALU.add)
                     nc.gpsimd.tensor_tensor(out=rstd[:], in0=ve[:], in1=nhalf[:], op=ALU.pow)

@@ -179,10 +179,12 @@ def tile_lstmcelllayernorm_w_kernel(
                     start=True,
                     stop=True,
                 )
-                nc.scalar.copy(out=bcast[:, NT * j : NT * (j + 1)], in_=ps[:])
+                if j % 2 == 0:
+                    nc.scalar.copy(out=bcast[:, NT * j : NT * (j + 1)], in_=ps[:])
+                else:
+                    nc.vector.tensor_copy(out=bcast[:, NT * j : NT * (j + 1)], in_=ps[:])
 
-        spread([0, 1, 2, 3, 4, 5])
-        extras = {1: [9, 10, 11], 2: [12, 13, 14], 3: [15, 16, 17], 4: [6, 7, 8]}
+        spread([0, 1, 2, 3, 4, 5, 9, 10, 11, 12, 13, 14, 15, 16, 17, 6, 7, 8])
         lnw = bcast[:, 12 * NT : 15 * NT]
         lnb = bcast[:, 15 * NT : 18 * NT]
 
@@ -247,8 +249,6 @@ def tile_lstmcelllayernorm_w_kernel(
                 if kg == KG - 1:
                     done.append(n0)
                 n0 += wd
-            if first == COL_I and kg in extras:
-                spread(extras[kg])
             if len(done) == 0:
                 continue
             if first == COL_I:

@@ -96,9 +96,10 @@ def tile_lstmcelllayernorm_w_kernel(
             steps.append((kg, COL_I, H))
         for kg in range(IF_JOINT, KG):
             steps.append((kg, COL_F, H))
-        for j in range(3):
-            for kg in range(KG):
-                steps.append((kg, COL_G + NT * j, NT))
+        for kg in range(KG):
+            steps.append((kg, COL_G, 2 * NT))
+        for kg in range(KG):
+            steps.append((kg, COL_G + 2 * NT, NT))
         for kg in range(KG):
             steps.append((kg, COL_O, 2 * NT))
         for kg in range(KG - 1):
@@ -200,10 +201,13 @@ def tile_lstmcelllayernorm_w_kernel(
         def cols(j):
             return slice(NT * j, NT * (j + 1))
 
-        def cell(j):
-            nc.vector.tensor_tensor(out=gg[:, cols(j)], in0=gg[:, cols(j)], in1=gi[:, cols(j)], op=ALU.mult)
-            nc.vector.tensor_tensor(out=gg[:, cols(j)], in0=gg[:, cols(j)], in1=gf[:, cols(j)], op=ALU.add)
-            nc.vector.bn_stats(out=stats[:, j, :], in_=gg[:, cols(j)])
+        def cell(js):
+            for j in js:
+                nc.vector.tensor_tensor(out=gg[:, cols(j)], in0=gg[:, cols(j)], in1=gi[:, cols(j)], op=ALU.mult)
+            for j in js:
+                nc.vector.tensor_tensor(out=gg[:, cols(j)], in0=gg[:, cols(j)], in1=gf[:, cols(j)], op=ALU.add)
+            for j in js:
+                nc.vector.bn_stats(out=stats[:, j, :], in_=gg[:, cols(j)])
 
         def hidden(c0, wd):
             nc.vector.tensor_tensor(out=go[:, c0 : c0 + wd], in0=go[:, c0 : c0 + wd], in1=th[:, c0 : c0 + wd], op=ALU.mult)
@@ -260,10 +264,10 @@ def tile_lstmcelllayernorm_w_kernel(
                 for j in range(3):
                     nc.vector.tensor_tensor(out=gf[:, cols(j)], in0=gf[:, cols(j)], in1=c_sb[:, cols(j)], op=ALU.mult)
             elif first >= COL_G:
-                j = (first - COL_G) // NT
-                preact(first, gg, COL_G, ACT.Tanh)
-                cell(j)
-                if j == 2:
+                for m0 in done:
+                    preact(m0, gg, COL_G, ACT.Tanh)
+                cell([(m0 - COL_G) // NT for m0 in done])
+                if first > COL_G:
                     nc.vector.bn_aggr(out=mv[:], in_=stats[:].rearrange("p a b -> p (a b)"))
                     nc.vector.tensor_scalar(out=ve[:], in0=mv[:, 1:2], scalar1=EPS, scalar2=None, op0=ALU.add)
                     nc.gpsimd.tensor_tensor(out=rstd[:], in0=ve[:], in1=nhalf[:], op=ALU.pow)

@@ -26,7 +26,7 @@ COL_F = H
 COL_O = 2 * H
 COL_G = 3 * H
 
-IF_JOINT = 5
+IF_JOINT = 7
 W_BUFS = {2 * H: 4, H: 4, 2 * NT: 5, NT: 10, NT // 2: 2}
 
 
@@ -39,6 +39,7 @@ def tile_lstmcelllayernorm_w_kernel(
         work = ctx.enter_context(tc.tile_pool(name="work", bufs=5))
         wpool = ctx.enter_context(tc.tile_pool(name="wpool", bufs=1))
         psum = ctx.enter_context(tc.psum_pool(name="psum", bufs=8))
+        ctx.enter_context(tc.manual_schedule(engines={mybir.EngineType.DVE}))
 
         ident = keep.tile([P, P], F32, name="ident")
         sel = keep.tile([P, 18], BF16, name="sel")
@@ -206,6 +207,8 @@ def tile_lstmcelllayernorm_w_kernel(
                 nc.vector.tensor_tensor(out=gg[:, cols(j)], in0=gg[:, cols(j)], in1=gi[:, cols(j)], op=ALU.mult)
             for j in js:
                 nc.vector.tensor_tensor(out=gg[:, cols(j)], in0=gg[:, cols(j)], in1=gf[:, cols(j)], op=ALU.add)
+
+        def statistics(js):
             for j in js:
                 nc.vector.bn_stats(out=stats[:, j, :], in_=gg[:, cols(j)])
 
@@ -257,17 +260,21 @@ def tile_lstmcelllayernorm_w_kernel(
                 continue
             if first == COL_I:
                 for m0 in done:
-                    preact(m0, gi, COL_I, ACT.Sigmoid)
-            elif first == COL_F:
-                for m0 in done:
-                    preact(m0, gf, COL_F, ACT.Sigmoid)
+                    if m0 < COL_F:
+                        preact(m0, gi, COL_I, ACT.Sigmoid)
+                    else:
+                        preact(m0, gf, COL_F, ACT.Sigmoid)
                 for j in range(3):
                     nc.vector.tensor_tensor(out=gf[:, cols(j)], in0=gf[:, cols(j)], in1=c_sb[:, cols(j)], op=ALU.mult)
             elif first >= COL_G:
                 for m0 in done:
                     preact(m0, gg, COL_G, ACT.Tanh)
-                cell([(m0 - COL_G) // NT for m0 in done])
-                if first > COL_G:
+                if first == COL_G:
+                    cell([0, 1])
+                else:
+                    statistics([0, 1])
+                    cell([2])
+                    statistics([2])
                     nc.vector.bn_aggr(out=mv[:], in_=stats[:].rearrange("p a b -> p (a b)"))
                     nc.vector.tensor_scalar(out=ve[:], in0=mv[:, 1:2], scalar1=EPS, scalar2=None, op0=ALU.add)
                     nc.gpsimd.tensor_tensor(out=rstd[:], in0=ve[:], in1=nhalf[:], op=ALU.pow)

@@ -27,7 +27,7 @@ COL_O = 2 * H
 COL_G = 3 * H
 
 IF_JOINT = 7
-W_BUFS = {2 * H: 4, H: 4, 2 * NT: 5, NT: 10, NT // 2: 2}
+W_BUFS = {2 * H: 7, H: 4, 2 * NT: 5, NT: 10, NT // 2: 2}
 
 
 def tile_lstmcelllayernorm_w_kernel(

@@ -27,7 +27,7 @@ COL_O = 2 * H
 COL_G = 3 * H
 
 IF_JOINT = 7
-W_BUFS = {2 * H: 7, H: 4, 2 * NT: 5, NT: 10, NT // 2: 2}
+W_BUFS = {2 * H: 7, H: 4, 2 * NT: 7, NT: 10, NT // 2: 2}
 
 
 def tile_lstmcelllayernorm_w_kernel(

from contextlib import ExitStack

import concourse.mybir as mybir
from concourse.masks import make_identity

F32 = mybir.dt.float32
BF16 = mybir.dt.bfloat16
U8 = mybir.dt.uint8
U32 = mybir.dt.uint32
I32 = mybir.dt.int32
FP8X4 = mybir.dt.float8_e4m3fn_x4
ALU = mybir.AluOpType
ACT = mybir.ActivationFunctionType

P = 128
I_DIM = 2048
H = 1536
EPS = 1e-5
NT = 512
KG_IH = 4
KG = 7
FLOPS = 2 * P * (I_DIM + H) * 4 * H

COL_I = 0
COL_F = H
COL_O = 2 * H
COL_G = 3 * H

IF_JOINT = 7
W_BUFS = {2 * H: 7, H: 4, 2 * NT: 7, NT: 10, NT // 2: 2}


def tile_lstmcelllayernorm_w_kernel(
    tc, x, h, c, W_ih_words, W_ih_scales, b_ih, W_hh_words, W_hh_scales, b_hh, ln_w, ln_b, out_0, out_1
):
    nc = tc.nc
    with ExitStack() as ctx:
        keep = ctx.enter_context(tc.tile_pool(name="keep", bufs=1))
        work = ctx.enter_context(tc.tile_pool(name="work", bufs=5))
        wpool = ctx.enter_context(tc.tile_pool(name="wpool", bufs=1))
        psum = ctx.enter_context(tc.psum_pool(name="psum", bufs=8))
        ctx.enter_context(tc.manual_schedule(engines={mybir.EngineType.DVE}))

        ident = keep.tile([P, P], F32, name="ident")
        sel = keep.tile([P, 18], BF16, name="sel")
        vecs = keep.tile([P, NT], BF16, name="vecs")
        nhalf = keep.tile([P, 1], F32, name="nhalf")
        xh = keep.tile([P, I_DIM + H], BF16, name="xh")
        grouped = keep.tile([P, I_DIM + H], BF16, name="grouped", align_bytes=64)
        codes = keep.tile([P, KG * P], U32, name="codes", align_bytes=64)
        xs = keep.tile([P, KG * P], U8, name="xs", align_bytes=64)
        planes_ih = keep.tile([P, 4 * H], U8, name="planes_ih", align_bytes=64)
        planes_hh = keep.tile([P, 4 * H], U8, name="planes_hh", align_bytes=64)
        bcast = keep.tile([P, 18 * NT], F32, name="bcast")
        c_sb = keep.tile([P, H], BF16, name="c_sb")
        stats = keep.tile([P, 3, 6], F32, name="stats")
        mv = keep.tile([P, 2], F32, name="mv")
        ve = keep.tile([P, 1], F32, name="ve")
        rstd = keep.tile([P, 1], F32, name="rstd")

        nc.sync.dma_start(out=xh[:, 0:I_DIM], in_=x)
        nc.sync.dma_start(out=xh[:, I_DIM : I_DIM + H], in_=h)

        nc.vector.memset(vecs[:], 0.0)
        nc.vector.memset(planes_ih[:].bitcast(I32), 0)
        nc.vector.memset(planes_hh[:].bitcast(I32), 0)
        make_identity(nc, ident[:])
        nc.gpsimd.memset(nhalf[:], -0.5)

        nc.scalar.dma_start(out=vecs[0:12, :], in_=b_ih.rearrange("(r n) -> r n", r=12))
        nc.scalar.dma_start(out=vecs[12:24, :], in_=b_hh.rearrange("(r n) -> r n", r=12))
        nc.scalar.dma_start(out=vecs[24:27, :], in_=ln_w.rearrange("(r n) -> r n", r=3))
        nc.scalar.dma_start(out=vecs[27:30, :], in_=ln_b.rearrange("(r n) -> r n", r=3))

        def load_scales(q, planes, scales, rows):
            if q < 2:
                nc.sync.dma_start(
                    out=planes[32 * q : 32 * q + rows, :].bitcast(I32),
                    in_=scales[:, 4 * q : 4 * q + 4, :].bitcast(I32),
                )
            else:
                nc.gpsimd.dma_start(
                    out=planes[32 * q : 32 * q + rows, :].bitcast(F32),
                    in_=scales[:, 4 * q : 4 * q + 4, :].bitcast(F32),
                )

        for q in range(4):
            load_scales(q, planes_ih, W_ih_scales, 16)
        for q in range(4):
            load_scales(q, planes_hh, W_hh_scales, 12)
        nc.sync.dma_start(out=c_sb[:], in_=c)

        steps = []
        for kg in range(IF_JOINT):
            steps.append((kg, COL_I, 2 * H))
        for kg in range(IF_JOINT, KG):
            steps.append((kg, COL_I, H))
        for kg in range(IF_JOINT, KG):
            steps.append((kg, COL_F, H))
        for kg in range(KG):
            steps.append((kg, COL_G, 2 * NT))
        for kg in range(KG):
            steps.append((kg, COL_G + 2 * NT, NT))
        for kg in range(KG):
            steps.append((kg, COL_O, 2 * NT))
        for kg in range(KG - 1):
            steps.append((kg, COL_O + 2 * NT, NT))
        for half in range(2):
            steps.append((KG - 1, COL_O + 2 * NT + (NT // 2) * half, NT // 2))

        w_tiles = {}
        taken = {}
        for width in W_BUFS:
            taken[width] = []
        issued = [0]

        def prefetch(n):
            for m in range(issued[0], len(steps)):
                kg, n0, width = steps[m]
                before = taken[width]
                if len(before) >= W_BUFS[width] and before[len(before) - W_BUFS[width]] >= n:
                    break
                words = W_ih_words[kg] if kg < KG_IH else W_hh_words[kg - KG_IH]
                flat = words.rearrange("p n t -> p (n t)")
                w = wpool.tile([P, width], U32, name="w%d" % width, tag="w%d" % width, bufs=W_BUFS[width], align_bytes=64)
                nc.sync.dma_start(out=w[:].bitcast(I32), in_=flat[:, 4 * n0 : 4 * (n0 + width)].bitcast(I32))
                w_tiles[m] = w
                before.append(m)
                issued[0] = m + 1

        prefetch(0)

        nc.vector.tensor_tensor(out=sel[:, 0:12], in0=ident[:, 0:12], in1=ident[:, 12:24], op=ALU.add)
        nc.vector.tensor_copy(out=sel[:, 12:18], in_=ident[:, 24:30])

        xw = xh[:].bitcast(F32)
        gw = grouped[:].bitcast(F32)
        tps = []
        for pr in range(4):
            tp = psum.tile([P, NT], F32, name="tp", tag="ps")
            tps.append(tp)
            for gl in range(2):
                g = 2 * pr + gl
                if g < KG:
                    for u in range(2):
                        nc.tensor.transpose(
                            out=tp[:, 256 * gl + 128 * u : 256 * gl + 128 * u + 128],
                            in_=xw[:, 256 * g + u : 256 * (g + 1) : 2],
                            identity=ident[:],
                        )

        def regroup(pr):
            ng = 2 if pr < 3 else 1
            nc.vector.tensor_copy(
                out=gw[:, 512 * pr : 512 * pr + 256 * ng].rearrange("p (g m u) -> p g m u", g=ng, u=2),
                in_=tps[pr][:, 0 : 256 * ng].rearrange("p (g u m) -> p g m u", g=ng, u=2),
            )

        def quantise(g0, ng):
            nc.vector.quantize_mx(
                out=codes[:, P * g0 : P * (g0 + ng)].bitcast(FP8X4),
                scales=xs[:, P * g0 : P * (g0 + ng)],
                in_=grouped[:, NT * g0 : NT * (g0 + ng)],
            )

        regroup(0)
        regroup(1)
        regroup(2)
        quantise(0, 4)
        regroup(3)
        quantise(4, 2)
        quantise(6, 1)

        def spread(js):
            for j in js:
                ps = psum.tile([P, NT], F32, name="ps", tag="ps")
                nc.tensor.matmul(
                    out=ps[:],
                    lhsT=sel[:, j : j + 1].to_broadcast([P, P]),
                    rhs=vecs[:],
                    start=True,
                    stop=True,
                )
                if j % 2 == 0:
                    nc.scalar.copy(out=bcast[:, NT * j : NT * (j + 1)], in_=ps[:])
                else:
                    nc.vector.tensor_copy(out=bcast[:, NT * j : NT * (j + 1)], in_=ps[:])

        spread([0, 1, 2, 3, 4, 5, 9, 10, 11, 12, 13, 14, 15, 16, 17, 6, 7, 8])
        lnw = bcast[:, 12 * NT : 15 * NT]
        lnb = bcast[:, 15 * NT : 18 * NT]

        def widths_of(n0):
            return NT // 2 if n0 >= COL_O + 2 * NT and n0 < COL_G else NT

        def preact(n0, dst, first, func):
            wd = widths_of(n0)
            d = dst[:, n0 - first : n0 - first + wd]
            nc.vector.tensor_tensor(out=d, in0=accs[n0][:, 0:wd], in1=bcast[:, n0 : n0 + wd], op=ALU.add)
            nc.scalar.activation(out=d, in_=d, func=func)

        def cols(j):
            return slice(NT * j, NT * (j + 1))

        def cell(js):
            for j in js:
                nc.vector.tensor_tensor(out=gg[:, cols(j)], in0=gg[:, cols(j)], in1=gi[:, cols(j)], op=ALU.mult)
            for j in js:
                nc.vector.tensor_tensor(out=gg[:, cols(j)], in0=gg[:, cols(j)], in1=gf[:, cols(j)], op=ALU.add)

        def statistics(js):
            for j in js:
                nc.vector.bn_stats(out=stats[:, j, :], in_=gg[:, cols(j)])

        def hidden(c0, wd):
            nc.vector.tensor_tensor(out=go[:, c0 : c0 + wd], in0=go[:, c0 : c0 + wd], in1=th[:, c0 : c0 + wd], op=ALU.mult)
            nc.sync.dma_start(out=out_0[:, c0 : c0 + wd], in_=go[:, c0 : c0 + wd])

        gi = work.tile([P, H], F32, name="gi", tag="work")
        gf = work.tile([P, H], F32, name="gf", tag="work")
        gg = work.tile([P, H], F32, name="gg", tag="work")
        tn = work.tile([P, H], F32, name="tn", tag="work")
        ct = work.tile([P, H], F32, name="ct", tag="work")
        th = None
        go = None

        accs = {}
        ct_stored = False
        for n in range(len(steps)):
            kg, first, width = steps[n]
            prefetch(n)
            if issued[0] == len(steps) and th is not None and not ct_stored:
                nc.sync.dma_start(out=out_1, in_=ct[:])
                ct_stored = True
            w = w_tiles[n]
            planes = planes_ih if kg < KG_IH else planes_hh
            k_off = 4 * (kg % KG_IH)
            n0 = first
            done = []
            for rep in range(12):
                if n0 >= first + width:
                    break
                wd = widths_of(n0)
                if kg == 0:
                    acc = psum.tile([P, NT], F32, name="acc", tag="ps")
                    accs[n0] = acc
                nc.tensor.matmul_mx(
                    out=accs[n0][:, 0:wd],
                    lhsT=codes[:, P * kg : P * (kg + 1)].bitcast(FP8X4),
                    lhsT_scale=xs[:, P * kg : P * (kg + 1)],
                    rhs=w[:, n0 - first : n0 - first + wd].bitcast(FP8X4),
                    rhs_scale=planes[k_off:P, n0 : n0 + wd],
                    start=(kg == 0),
                    stop=(kg == KG - 1),
                )
                if kg == KG - 1:
                    done.append(n0)
                n0 += wd
            if len(done) == 0:
                continue
            if first == COL_I:
                for m0 in done:
                    if m0 < COL_F:
                        preact(m0, gi, COL_I, ACT.Sigmoid)
                    else:
                        preact(m0, gf, COL_F, ACT.Sigmoid)
                for j in range(3):
                    nc.vector.tensor_tensor(out=gf[:, cols(j)], in0=gf[:, cols(j)], in1=c_sb[:, cols(j)], op=ALU.mult)
            elif first >= COL_G:
                for m0 in done:
                    preact(m0, gg, COL_G, ACT.Tanh)
                if first == COL_G:
                    cell([0, 1])
                else:
                    statistics([0, 1])
                    cell([2])
                    statistics([2])
                    nc.vector.bn_aggr(out=mv[:], in_=stats[:].rearrange("p a b -> p (a b)"))
                    nc.vector.tensor_scalar(out=ve[:], in0=mv[:, 1:2], scalar1=EPS, scalar2=None, op0=ALU.add)
                    nc.gpsimd.tensor_tensor(out=rstd[:], in0=ve[:], in1=nhalf[:], op=ALU.pow)
                    nc.vector.scalar_tensor_tensor(
                        out=tn[:], in0=gg[:], scalar=mv[:, 0:1], in1=lnw, op0=ALU.subtract, op1=ALU.mult
                    )
                    th = work.tile([P, H], F32, name="th", tag="work")
                    go = work.tile([P, H], F32, name="go", tag="work")
                    for jj in range(3):
                        nc.vector.scalar_tensor_tensor(
                            out=ct[:, cols(jj)],
                            in0=tn[:, cols(jj)],
                            scalar=rstd[:, 0:1],
                            in1=lnb[:, cols(jj)],
                            op0=ALU.mult,
                            op1=ALU.add,
                        )
                        nc.scalar.activation(out=th[:, cols(jj)], in_=ct[:, cols(jj)], func=ACT.Tanh)
            else:
                for m0 in done:
                    preact(m0, go, COL_O, ACT.Sigmoid)
                if first == COL_O:
                    hidden(0, NT)
                    hidden(NT, NT)
        hidden(2 * NT, NT // 2)
        hidden(2 * NT + NT // 2, NT // 2)
